import numpy as np
import ml_dtypes

BF16 = ml_dtypes.bfloat16


def bf(x):
    return np.asarray(x, np.float32).astype(BF16)


def f32(x):
    return np.asarray(x, np.float32)


def f64(x):
    return np.asarray(x).astype(np.float64)


def striped(idx):
    return np.tile(idx.reshape(-1, 16).T, (8, 1))


D, BS, NSP, R, S, N = 128, 128, 4, 2, 512, 1024
SCALE = 1.0 / np.sqrt(D)


def setup_inputs():
    blocks = np.random.permutation(np.tile(np.arange(NSP), R))
    idx = (blocks[:, None] * BS + np.arange(BS)[None, :]).reshape(-1)
    return {"q": bf(0.5 * np.random.standard_normal((D, S))), "table": bf(np.random.standard_normal((D, S))), "offs": striped(idx)}


def reference(q, table, offs):
    idx = offs[:16].T.reshape(-1)
    picked = f64(table)[:, idx].reshape(D, NSP, R * BS)
    qb = f64(q).reshape(D, NSP, BS)
    scores = np.einsum("dni,dnt->int", qb, picked).reshape(BS, N)
    return np.exp(SCALE * scores)

@@ -1,0 +1,47 @@
+import math
+
+import concourse.mybir as mybir
+
+BF16, F32, U16 = mybir.dt.bfloat16, mybir.dt.float32, mybir.dt.uint16
+EXP = mybir.ActivationFunctionType.Exp
+
+D = 128
+KEYS = 512
+BLOCK = 128
+N_BLOCKS = 4
+PICKED = 256
+N = N_BLOCKS * PICKED
+PER_COLUMN = 16
+SCALE = 1.0 / math.sqrt(D)
+
+FLOPS = 2 * D * BLOCK * N
+
+
+def tile_multiheadsparseattn_kernel(tc, q, table, offs, out):
+    nc = tc.nc
+    with (
+        tc.tile_pool(name="held", bufs=1) as held,
+        tc.tile_pool(name="ring", bufs=N_BLOCKS) as ring,
+        tc.psum_pool(name="psum", bufs=N_BLOCKS) as psum,
+    ):
+        keys = held.tile([D, KEYS], BF16, name="keys")
+        nc.sync.dma_start(keys[:, 0 : KEYS // 2], table[:, 0 : KEYS // 2])
+        nc.sync.dma_start(keys[:, KEYS // 2 :], table[:, KEYS // 2 :])
+        offsets = held.tile([128, N // PER_COLUMN], U16, name="offsets")
+        nc.sync.dma_start(offsets[:], offs)
+        queries = held.tile([D, N_BLOCKS * BLOCK], BF16, name="queries")
+        nc.sync.dma_start(queries[:], q)
+
+        columns = PICKED // PER_COLUMN
+        for n in range(N_BLOCKS):
+            scores = psum.tile([BLOCK, PICKED], F32, name="scores")
+            nc.tensor.matmul(
+                scores[:],
+                queries[:, n * BLOCK : (n + 1) * BLOCK],
+                keys[:].indirect(offsets[:, n * columns : (n + 1) * columns]),
+                start=True,
+                stop=True,
+            )
+            weights = ring.tile([BLOCK, PICKED], F32, name="weights")
+            nc.scalar.activation(weights[:], scores[:], EXP, scale=SCALE)
+            nc.sync.dma_start(out[:, n * PICKED : (n + 1) * PICKED], weights[:])

@@ -13,6 +13,8 @@ PICKED = 256
 N = N_BLOCKS * PICKED
 PER_COLUMN = 16
 SCALE = 1.0 / math.sqrt(D)
+WARM_COLUMNS = 512
+WARM_MATMULS = 3
 
 FLOPS = 2 * D * BLOCK * N
 
@@ -22,26 +24,40 @@ def tile_multiheadsparseattn_kernel(tc, q, table, offs, out):
     with (
         tc.tile_pool(name="held", bufs=1) as held,
         tc.tile_pool(name="ring", bufs=N_BLOCKS) as ring,
-        tc.psum_pool(name="psum", bufs=N_BLOCKS) as psum,
+        tc.psum_pool(name="psum", bufs=N_BLOCKS + 2) as psum,
+        tc.psum_pool(name="warm", bufs=1) as warm,
     ):
         keys = held.tile([D, KEYS], BF16, name="keys")
-        nc.sync.dma_start(keys[:, 0 : KEYS // 2], table[:, 0 : KEYS // 2])
-        nc.sync.dma_start(keys[:, KEYS // 2 :], table[:, KEYS // 2 :])
+        nc.sync.dma_start(keys[:], table)
+        queries = held.tile([D, N_BLOCKS * BLOCK], BF16, name="queries")
+        nc.sync.dma_start(queries[:, 0:BLOCK], q[:, 0:BLOCK])
         offsets = held.tile([128, N // PER_COLUMN], U16, name="offsets")
         nc.sync.dma_start(offsets[:], offs)
-        queries = held.tile([D, N_BLOCKS * BLOCK], BF16, name="queries")
-        nc.sync.dma_start(queries[:], q)
+        nc.sync.dma_start(queries[:, BLOCK:], q[:, BLOCK:])
+
+        zeros = held.tile([D, BLOCK], BF16, name="zeros")
+        nc.vector.memset(zeros[:], 0.0)
+        unused = warm.tile([BLOCK, WARM_COLUMNS], F32, name="unused")
+        for w in range(WARM_MATMULS):
+            nc.tensor.matmul(
+                unused[:], zeros[:], zeros[:, 0:1].to_broadcast([D, WARM_COLUMNS]), start=True, stop=True
+            )
 
         columns = PICKED // PER_COLUMN
         for n in range(N_BLOCKS):
-            scores = psum.tile([BLOCK, PICKED], F32, name="scores")
-            nc.tensor.matmul(
-                scores[:],
-                queries[:, n * BLOCK : (n + 1) * BLOCK],
-                keys[:].indirect(offsets[:, n * columns : (n + 1) * columns]),
-                start=True,
-                stop=True,
-            )
             weights = ring.tile([BLOCK, PICKED], F32, name="weights")
-            nc.scalar.activation(weights[:], scores[:], EXP, scale=SCALE)
+            pieces = 2
+            width = PICKED // pieces
+            step = columns // pieces
+            for p in range(pieces):
+                first = n * columns + p * step
+                scores = psum.tile([BLOCK, width], F32, name="scores")
+                nc.tensor.matmul(
+                    scores[:],
+                    queries[:, n * BLOCK : (n + 1) * BLOCK],
+                    keys[:].indirect(offsets[:, first : first + step]),
+                    start=True,
+                    stop=True,
+                )
+                nc.scalar.activation(weights[:, p * width : (p + 1) * width], scores[:], EXP, scale=SCALE)
             nc.sync.dma_start(out[:, n * PICKED : (n + 1) * PICKED], weights[:])

import math

import concourse.mybir as mybir

BF16, F32, U16 = mybir.dt.bfloat16, mybir.dt.float32, mybir.dt.uint16
EXP = mybir.ActivationFunctionType.Exp

D = 128
KEYS = 512
BLOCK = 128
N_BLOCKS = 4
PICKED = 256
N = N_BLOCKS * PICKED
PER_COLUMN = 16
SCALE = 1.0 / math.sqrt(D)
WARM_COLUMNS = 512
WARM_MATMULS = 3

FLOPS = 2 * D * BLOCK * N


def tile_multiheadsparseattn_kernel(tc, q, table, offs, out):
    nc = tc.nc
    with (
        tc.tile_pool(name="held", bufs=1) as held,
        tc.tile_pool(name="ring", bufs=N_BLOCKS) as ring,
        tc.psum_pool(name="psum", bufs=N_BLOCKS + 2) as psum,
        tc.psum_pool(name="warm", bufs=1) as warm,
    ):
        keys = held.tile([D, KEYS], BF16, name="keys")
        nc.sync.dma_start(keys[:], table)
        queries = held.tile([D, N_BLOCKS * BLOCK], BF16, name="queries")
        nc.sync.dma_start(queries[:, 0:BLOCK], q[:, 0:BLOCK])
        offsets = held.tile([128, N // PER_COLUMN], U16, name="offsets")
        nc.sync.dma_start(offsets[:], offs)
        nc.sync.dma_start(queries[:, BLOCK:], q[:, BLOCK:])

        zeros = held.tile([D, BLOCK], BF16, name="zeros")
        nc.vector.memset(zeros[:], 0.0)
        unused = warm.tile([BLOCK, WARM_COLUMNS], F32, name="unused")
        for w in range(WARM_MATMULS):
            nc.tensor.matmul(
                unused[:], zeros[:], zeros[:, 0:1].to_broadcast([D, WARM_COLUMNS]), start=True, stop=True
            )

        columns = PICKED // PER_COLUMN
        for n in range(N_BLOCKS):
            weights = ring.tile([BLOCK, PICKED], F32, name="weights")
            pieces = 2
            width = PICKED // pieces
            step = columns // pieces
            for p in range(pieces):
                first = n * columns + p * step
                scores = psum.tile([BLOCK, width], F32, name="scores")
                nc.tensor.matmul(
                    scores[:],
                    queries[:, n * BLOCK : (n + 1) * BLOCK],
                    keys[:].indirect(offsets[:, first : first + step]),
                    start=True,
                    stop=True,
                )
                nc.scalar.activation(weights[:, p * width : (p + 1) * width], scores[:], EXP, scale=SCALE)
            nc.sync.dma_start(out[:, n * PICKED : (n + 1) * PICKED], weights[:])
